import numpy as np
import ml_dtypes


def mxq(x, axis, fmt="e4m3"):
    dtype, down = {"e4m3": (ml_dtypes.float8_e4m3fn, 7), "e5m2": (ml_dtypes.float8_e5m2, 14)}[fmt]
    v = np.moveaxis(np.asarray(x, np.float32).astype(ml_dtypes.bfloat16).astype(np.float64), axis, -1)
    blocks = v.reshape(v.shape[:-1] + (-1, 32))
    amax = np.abs(blocks).max(-1, keepdims=True)
    byte = np.maximum(np.where(amax > 0, np.frexp(amax)[1] - 1 + 127, 0) - down, 1)
    scale = np.exp2(byte - 127.0)
    codes = (blocks / scale).astype(np.float32).astype(dtype).astype(np.float64)
    return np.moveaxis((codes * scale).reshape(v.shape), -1, axis)


WIDE = False


def mx_kscale(k):
    if not WIDE:
        return np.ones(k)
    levels = np.array([20, -20, 10, -10, 0])
    a = np.random.permutation(np.resize(levels, k // 512 * 4)).reshape(k // 512, 4)
    idx = np.arange(k)
    return np.exp2(a[idx // 512, idx % 128 // 32])


BF16 = ml_dtypes.bfloat16


def bf(x):
    return np.asarray(x, np.float32).astype(BF16)


def f64(x):
    return np.asarray(x).astype(np.float64)


B, HH, WW, C, NH, KD, WS, SS = 1, 64, 64, 512, 8, 64, 8, 4
GH, GW, T, F = HH // WS, WW // WS, WS * WS, NH * KD
N = B * GH * GW


def merge_windows(p):
    last = p.shape[-1]
    m = p.reshape(B, GH, GW, WS, WS, last).swapaxes(2, 3).reshape(B, HH, WW, last)
    return np.roll(m, shift=(SS, SS), axis=(1, 2))


def split_windows(g):
    last = g.shape[-1]
    m = np.roll(g, shift=(-SS, -SS), axis=(1, 2))
    return m.reshape(B, GH, WS, GW, WS, last).swapaxes(2, 3).reshape(N * T, last)


def setup_inputs():
    s = mx_kscale(N * T)
    s_win = s.reshape(N, T, 1, 1)
    s_img = merge_windows(s.reshape(N * T, 1))
    attn_ctx = np.random.standard_normal((N, T, NH, KD)) * 0.4 * s_win
    x = np.random.standard_normal((B, HH, WW, C))
    wo = np.random.standard_normal((NH, KD, C)) * 2.0 / np.sqrt(F)
    bo = np.random.standard_normal(C) * 0.3
    g = np.random.standard_normal((B, HH, WW, C)) * np.exp2(np.random.randint(-12, 1, (B, HH, WW, 1))) / s_img
    return {"attn_ctx": bf(attn_ctx), "x": bf(x), "wo": bf(wo), "bo": bf(bo), "grad_out": bf(g)}


def reference(attn_ctx, x, wo, bo, grad_out):
    o = f64(attn_ctx).reshape(N * T, F)
    gw = split_windows(f64(grad_out))
    d = mxq(o, 0, "e4m3").T @ mxq(gw, 0, "e5m2")
    return d.reshape(NH, KD, C)

@@ -1,0 +1,130 @@
+from contextlib import ExitStack
+
+import concourse.mybir as mybir
+
+BF16 = mybir.dt.bfloat16
+F32 = mybir.dt.float32
+U32 = mybir.dt.uint32
+U8 = mybir.dt.uint8
+E4M3X4 = mybir.dt.float8_e4m3fn_x4
+E5M2X4 = mybir.dt.float8_e5m2_x4
+
+P = 128
+PACK = 4
+SIDE = 64
+WS = 8
+SHIFT = 4
+GRID = SIDE // WS
+F = 512
+C = 512
+PASSES = GRID
+M_TILES = F // P
+
+FLOPS = 2 * SIDE * SIDE * F * C
+BYTES = SIDE * SIDE * (F + C) * 2 + F * C * 4
+
+
+def unwrapped(first, count, step):
+    first = first % SIDE
+    head = min(count, SIDE - first)
+    pieces = [(0, first, head)]
+    if head < count:
+        pieces.append((head, 0, count - head))
+    assert all(v % step == 0 for piece in pieces for v in piece)
+    return pieces
+
+
+def tile_windowattentionblock_pb_kernel(tc, attn_ctx, x, wo, bo, grad_out, out):
+    nc = tc.nc
+    attn_windows = attn_ctx.rearrange("(gi gj) (y j) h d -> gj gi y (j h d)", gj=GRID, j=PACK)
+    image = grad_out[0]
+    out_rows = out.rearrange("h d c -> (h d) c")
+
+    with ExitStack() as ctx:
+        raw = ctx.enter_context(tc.tile_pool(name="raw", bufs=PASSES))
+        grouped = ctx.enter_context(tc.tile_pool(name="grouped", bufs=3))
+        keep = ctx.enter_context(tc.tile_pool(name="keep", bufs=1))
+        psum = ctx.enter_context(tc.psum_pool(name="psum", bufs=1))
+        results = ctx.enter_context(tc.tile_pool(name="results", bufs=M_TILES))
+
+        a_codes = keep.tile([P, PASSES, F], U32, align_bytes=64)
+        a_scales = keep.tile([P, PASSES, F], U8, align_bytes=64)
+        g_codes = keep.tile([P, PASSES, C], U32, align_bytes=64)
+        g_scales = keep.tile([P, PASSES, C], U8, align_bytes=64)
+        acc = [psum.tile([P, C], F32, name="acc%d" % m) for m in range(M_TILES)]
+
+        a_raw = []
+        g_raw = []
+        for gj in range(PASSES):
+            a_tile = raw.tile([P, PACK, F], BF16, name="a_raw")
+            nc.sync.dma_start(out=a_tile[:].rearrange("p j f -> p (j f)"), in_=attn_windows[gj])
+            a_raw.append(a_tile)
+
+            g_tile = raw.tile([P, PACK, C], BF16, name="g_raw")
+            g_flat = g_tile[:].rearrange("p j c -> p (j c)")
+            for u0, row0, rows in unwrapped(SHIFT, SIDE, PACK):
+                for v0, col0, cols in unwrapped(gj * WS + SHIFT, WS, PACK):
+                    pixels = image[row0 : row0 + rows, col0 : col0 + cols, :]
+                    if cols == WS:
+                        nc.sync.dma_start(out=g_flat[2 * u0 : 2 * (u0 + rows), :], in_=pixels)
+                    else:
+                        nc.sync.dma_start(
+                            out=g_flat[2 * u0 + v0 // PACK : 2 * (u0 + rows) : 2, :],
+                            in_=pixels.rearrange("i j c -> i (j c)"),
+                        )
+            g_raw.append(g_tile)
+
+        a_grouped = {}
+        g_grouped = {}
+
+        def regroup(gj):
+            a_grouped[gj] = grouped.tile([P, F, PACK], BF16, name="a_grouped", align_bytes=64)
+            nc.scalar.copy(
+                out=a_grouped[gj][:].rearrange("p (b i) j -> p b j i", i=4),
+                in_=a_raw[gj][:].rearrange("p j (b i) -> p b j i", i=4),
+            )
+            g_grouped[gj] = grouped.tile([P, C, PACK], BF16, name="g_grouped", align_bytes=64)
+            nc.vector.tensor_copy(
+                out=g_grouped[gj][:].rearrange("p (b i) j -> p b j i", i=4),
+                in_=g_raw[gj][:].rearrange("p j (b i) -> p b j i", i=4),
+            )
+
+        def quantise(gj):
+            nc.vector.quantize_mx(
+                out=g_codes[:, gj, :].bitcast(E5M2X4),
+                scales=g_scales[:, gj, :],
+                in_=g_grouped[gj][:].rearrange("p c j -> p (c j)"),
+            )
+            nc.vector.quantize_mx(
+                out=a_codes[:, gj, :].bitcast(E4M3X4),
+                scales=a_scales[:, gj, :],
+                in_=a_grouped[gj][:].rearrange("p f j -> p (f j)"),
+            )
+
+        def multiply(gj):
+            for m in range(M_TILES):
+                f_cols = slice(m * P, (m + 1) * P)
+                nc.tensor.matmul_mx(
+                    out=acc[m][:],
+                    lhsT=a_codes[:, gj, f_cols].bitcast(E4M3X4),
+                    lhsT_scale=a_scales[:, gj, f_cols],
+                    rhs=g_codes[:, gj, :].bitcast(E5M2X4),
+                    rhs_scale=g_scales[:, gj, :],
+                    start=(gj == 0),
+                    stop=(gj == PASSES - 1),
+                )
+
+        regroup(0)
+        for gj in range(PASSES):
+            if gj + 1 < PASSES:
+                regroup(gj + 1)
+            quantise(gj)
+            multiply(gj)
+
+        for m in range(M_TILES):
+            result = results.tile([P, C], F32, name="result")
+            if m % 2 == 0:
+                nc.scalar.copy(out=result[:], in_=acc[m][:])
+            else:
+                nc.vector.tensor_copy(out=result[:], in_=acc[m][:])
+            nc.sync.dma_start(out=out_rows[m * P : (m + 1) * P, :], in_=result[:])

@@ -1,6 +1,7 @@
 from contextlib import ExitStack
 
 import concourse.mybir as mybir
+from concourse.masks import make_identity
 
 BF16 = mybir.dt.bfloat16
 F32 = mybir.dt.float32
@@ -19,33 +20,59 @@ F = 512
 C = 512
 PASSES = GRID
 M_TILES = F // P
+RUNS = SIDE // PACK
+HALVES = 2
+HALF_C = C // HALVES
+WORDS = HALF_C // 2
 
 FLOPS = 2 * SIDE * SIDE * F * C
 BYTES = SIDE * SIDE * (F + C) * 2 + F * C * 4
 
 
-def unwrapped(first, count, step):
-    first = first % SIDE
-    head = min(count, SIDE - first)
-    pieces = [(0, first, head)]
-    if head < count:
-        pieces.append((head, 0, count - head))
-    assert all(v % step == 0 for piece in pieces for v in piece)
-    return pieces
-
-
 def tile_windowattentionblock_pb_kernel(tc, attn_ctx, x, wo, bo, grad_out, out):
     nc = tc.nc
-    attn_windows = attn_ctx.rearrange("(gi gj) (y j) h d -> gj gi y (j h d)", gj=GRID, j=PACK)
-    image = grad_out[0]
+    attn_rows = attn_ctx.rearrange("(gi gj) (y j) h d -> gi (gj y) (j h d)", gj=GRID, j=PACK)
+    image_runs = grad_out[0].rearrange("i (q j) c -> i q (j c)", j=PACK)
     out_rows = out.rearrange("h d c -> (h d) c")
 
     with ExitStack() as ctx:
+        ctx.enter_context(tc.manual_schedule())
+        const = ctx.enter_context(tc.tile_pool(name="const", bufs=1))
         raw = ctx.enter_context(tc.tile_pool(name="raw", bufs=PASSES))
+        turned = ctx.enter_context(tc.tile_pool(name="turned", bufs=2))
         grouped = ctx.enter_context(tc.tile_pool(name="grouped", bufs=3))
         keep = ctx.enter_context(tc.tile_pool(name="keep", bufs=1))
         psum = ctx.enter_context(tc.psum_pool(name="psum", bufs=1))
         results = ctx.enter_context(tc.tile_pool(name="results", bufs=M_TILES))
+
+        a_raw = []
+        g_raw = []
+        for gi in range(PASSES):
+            a_tile = raw.tile([P, PACK, F], BF16, name="a_raw")
+            nc.sync.dma_start(out=a_tile[:].rearrange("p j f -> p (j f)"), in_=attn_rows[gi])
+            a_raw.append(a_tile)
+            g_tile = raw.tile([P, PACK * C], BF16, name="g_raw")
+            first = (gi * WS + SHIFT) % SIDE
+            head = min(WS, SIDE - first)
+            nc.sync.dma_start(
+                out=g_tile[0 : head * RUNS, :],
+                in_=image_runs[first : first + head].rearrange("i q e -> (i q) e"),
+            )
+            if head < WS:
+                nc.sync.dma_start(
+                    out=g_tile[head * RUNS : P, :],
+                    in_=image_runs[0 : WS - head].rearrange("i q e -> (i q) e"),
+                )
+            g_raw.append(g_tile)
+
+        identity = const.tile([P, P], F32)
+        make_identity(nc, identity[:])
+        to_window = const.tile([P, P], F32)
+        image_cols = identity[:].rearrange("k (ti g e) -> k g ti e", g=GRID, e=2)
+        window_cols = to_window[:].rearrange("k (gj ti th) -> k gj ti th", ti=WS, th=2)
+        nc.vector.tensor_copy(out=window_cols[:, :, :, 0], in_=image_cols[:, :, :, 1])
+        nc.vector.tensor_copy(out=window_cols[:, 0 : GRID - 1, :, 1], in_=image_cols[:, 1:GRID, :, 0])
+        nc.vector.tensor_copy(out=window_cols[:, GRID - 1, :, 1], in_=image_cols[:, 0, :, 0])
 
         a_codes = keep.tile([P, PASSES, F], U32, align_bytes=64)
         a_scales = keep.tile([P, PASSES, F], U8, align_bytes=64)
@@ -53,73 +80,73 @@ def tile_windowattentionblock_pb_kernel(tc, attn_ctx, x, wo, bo, grad_out, out):
         g_scales = keep.tile([P, PASSES, C], U8, align_bytes=64)
         acc = [psum.tile([P, C], F32, name="acc%d" % m) for m in range(M_TILES)]
 
-        a_raw = []
-        g_raw = []
-        for gj in range(PASSES):
-            a_tile = raw.tile([P, PACK, F], BF16, name="a_raw")
-            nc.sync.dma_start(out=a_tile[:].rearrange("p j f -> p (j f)"), in_=attn_windows[gj])
-            a_raw.append(a_tile)
-
-            g_tile = raw.tile([P, PACK, C], BF16, name="g_raw")
-            g_flat = g_tile[:].rearrange("p j c -> p (j c)")
-            for u0, row0, rows in unwrapped(SHIFT, SIDE, PACK):
-                for v0, col0, cols in unwrapped(gj * WS + SHIFT, WS, PACK):
-                    pixels = image[row0 : row0 + rows, col0 : col0 + cols, :]
-                    if cols == WS:
-                        nc.sync.dma_start(out=g_flat[2 * u0 : 2 * (u0 + rows), :], in_=pixels)
-                    else:
-                        nc.sync.dma_start(
-                            out=g_flat[2 * u0 + v0 // PACK : 2 * (u0 + rows) : 2, :],
-                            in_=pixels.rearrange("i j c -> i (j c)"),
-                        )
-            g_raw.append(g_tile)
-
+        g_turned = {}
         a_grouped = {}
         g_grouped = {}
 
-        def regroup(gj):
-            a_grouped[gj] = grouped.tile([P, F, PACK], BF16, name="a_grouped", align_bytes=64)
-            nc.scalar.copy(
-                out=a_grouped[gj][:].rearrange("p (b i) j -> p b j i", i=4),
-                in_=a_raw[gj][:].rearrange("p j (b i) -> p b j i", i=4),
-            )
-            g_grouped[gj] = grouped.tile([P, C, PACK], BF16, name="g_grouped", align_bytes=64)
+        def turn(gi):
+            words = g_raw[gi][:].bitcast(F32).rearrange("p (j h w) -> p j h w", j=PACK, h=HALVES)
+            g_turned[gi] = turned.tile([P, HALVES, PACK, P], F32, name="g_turned")
+            for h in range(HALVES):
+                bank = psum.tile([P, PACK, P], F32, name="turn%d" % h)
+                for j in range(PACK):
+                    nc.tensor.transpose(bank[:, j, :], words[:, j, h, :], to_window[:])
+                if h == 0:
+                    nc.scalar.copy(out=g_turned[gi][:, h], in_=bank[:])
+                else:
+                    nc.vector.tensor_copy(out=g_turned[gi][:, h], in_=bank[:])
+
+        def turn_back(gi):
+            g_grouped[gi] = grouped.tile([P, C, PACK], BF16, name="g_grouped", align_bytes=64)
+            for h in range(HALVES):
+                bank = psum.tile([P, PACK, P], F32, name="back%d" % h)
+                for j in range(PACK):
+                    nc.tensor.transpose(bank[:, j, :], g_turned[gi][:, h, j, :], identity[:])
+                nc.scalar.copy(
+                    out=g_grouped[gi][:, h * HALF_C : (h + 1) * HALF_C, :],
+                    in_=bank[:].bitcast(BF16).rearrange("p j c -> p c j"),
+                )
+
+        def regroup_attn(gi):
+            a_grouped[gi] = grouped.tile([P, F, PACK], BF16, name="a_grouped", align_bytes=64)
             nc.vector.tensor_copy(
-                out=g_grouped[gj][:].rearrange("p (b i) j -> p b j i", i=4),
-                in_=g_raw[gj][:].rearrange("p j (b i) -> p b j i", i=4),
+                out=a_grouped[gi][:].rearrange("p (b i) j -> p b j i", i=4),
+                in_=a_raw[gi][:].rearrange("p j (b i) -> p b j i", i=4),
             )
 
-        def quantise(gj):
+        def quantise(gi):
             nc.vector.quantize_mx(
-                out=g_codes[:, gj, :].bitcast(E5M2X4),
-                scales=g_scales[:, gj, :],
-                in_=g_grouped[gj][:].rearrange("p c j -> p (c j)"),
+                out=a_codes[:, gi, :].bitcast(E4M3X4),
+                scales=a_scales[:, gi, :],
+                in_=a_grouped[gi][:].rearrange("p f j -> p (f j)"),
             )
             nc.vector.quantize_mx(
-                out=a_codes[:, gj, :].bitcast(E4M3X4),
-                scales=a_scales[:, gj, :],
-                in_=a_grouped[gj][:].rearrange("p f j -> p (f j)"),
+                out=g_codes[:, gi, :].bitcast(E5M2X4),
+                scales=g_scales[:, gi, :],
+                in_=g_grouped[gi][:].rearrange("p c j -> p (c j)"),
             )
 
-        def multiply(gj):
+        def multiply(gi):
             for m in range(M_TILES):
                 f_cols = slice(m * P, (m + 1) * P)
                 nc.tensor.matmul_mx(
                     out=acc[m][:],
-                    lhsT=a_codes[:, gj, f_cols].bitcast(E4M3X4),
-                    lhsT_scale=a_scales[:, gj, f_cols],
-                    rhs=g_codes[:, gj, :].bitcast(E5M2X4),
-                    rhs_scale=g_scales[:, gj, :],
-                    start=(gj == 0),
-                    stop=(gj == PASSES - 1),
+                    lhsT=a_codes[:, gi, f_cols].bitcast(E4M3X4),
+                    lhsT_scale=a_scales[:, gi, f_cols],
+                    rhs=g_codes[:, gi, :].bitcast(E5M2X4),
+                    rhs_scale=g_scales[:, gi, :],
+                    start=(gi == 0),
+                    stop=(gi == PASSES - 1),
                 )
 
-        regroup(0)
-        for gj in range(PASSES):
-            if gj + 1 < PASSES:
-                regroup(gj + 1)
-            quantise(gj)
-            multiply(gj)
+        stages = [turn, turn_back, quantise, multiply]
+        for step in range(PASSES + len(stages) - 1):
+            for lag, stage in enumerate(stages):
+                gi = step - lag
+                if 0 <= gi < PASSES:
+                    stage(gi)
+                    if stage is turn:
+                        regroup_attn(gi)
 
         for m in range(M_TILES):
             result = results.tile([P, C], F32, name="result")

@@ -48,9 +48,6 @@ def tile_windowattentionblock_pb_kernel(tc, attn_ctx, x, wo, bo, grad_out, out):
         a_raw = []
         g_raw = []
         for gi in range(PASSES):
-            a_tile = raw.tile([P, PACK, F], BF16, name="a_raw")
-            nc.sync.dma_start(out=a_tile[:].rearrange("p j f -> p (j f)"), in_=attn_rows[gi])
-            a_raw.append(a_tile)
             g_tile = raw.tile([P, PACK * C], BF16, name="g_raw")
             first = (gi * WS + SHIFT) % SIDE
             head = min(WS, SIDE - first)
@@ -64,6 +61,9 @@ def tile_windowattentionblock_pb_kernel(tc, attn_ctx, x, wo, bo, grad_out, out):
                     in_=image_runs[0 : WS - head].rearrange("i q e -> (i q) e"),
                 )
             g_raw.append(g_tile)
+            a_tile = raw.tile([P, PACK, F], BF16, name="a_raw")
+            nc.sync.dma_start(out=a_tile[:].rearrange("p j f -> p (j f)"), in_=attn_rows[gi])
+            a_raw.append(a_tile)
 
         identity = const.tile([P, P], F32)
         make_identity(nc, identity[:])
@@ -92,9 +92,9 @@ def tile_windowattentionblock_pb_kernel(tc, attn_ctx, x, wo, bo, grad_out, out):
                 for j in range(PACK):
                     nc.tensor.transpose(bank[:, j, :], words[:, j, h, :], to_window[:])
                 if h == 0:
-                    nc.scalar.copy(out=g_turned[gi][:, h], in_=bank[:])
-                else:
                     nc.vector.tensor_copy(out=g_turned[gi][:, h], in_=bank[:])
+                else:
+                    nc.scalar.copy(out=g_turned[gi][:, h], in_=bank[:])
 
         def turn_back(gi):
             g_grouped[gi] = grouped.tile([P, C, PACK], BF16, name="g_grouped", align_bytes=64)
@@ -114,12 +114,14 @@ def tile_windowattentionblock_pb_kernel(tc, attn_ctx, x, wo, bo, grad_out, out):
                 in_=a_raw[gi][:].rearrange("p j (b i) -> p b j i", i=4),
             )
 
-        def quantise(gi):
+        def quantise_attn(gi):
             nc.vector.quantize_mx(
                 out=a_codes[:, gi, :].bitcast(E4M3X4),
                 scales=a_scales[:, gi, :],
                 in_=a_grouped[gi][:].rearrange("p f j -> p (f j)"),
             )
+
+        def quantise_grad(gi):
             nc.vector.quantize_mx(
                 out=g_codes[:, gi, :].bitcast(E5M2X4),
                 scales=g_scales[:, gi, :],
@@ -139,14 +141,18 @@ def tile_windowattentionblock_pb_kernel(tc, attn_ctx, x, wo, bo, grad_out, out):
                     stop=(gi == PASSES - 1),
                 )
 
-        stages = [turn, turn_back, quantise, multiply]
-        for step in range(PASSES + len(stages) - 1):
-            for lag, stage in enumerate(stages):
-                gi = step - lag
-                if 0 <= gi < PASSES:
-                    stage(gi)
-                    if stage is turn:
-                        regroup_attn(gi)
+        for step in range(PASSES + 3):
+            if step < PASSES:
+                turn(step)
+            if 0 <= step - 3 < PASSES:
+                multiply(step - 3)
+            if step < PASSES:
+                regroup_attn(step)
+            if 0 <= step - 1 < PASSES:
+                quantise_grad(step - 1)
+            if step < PASSES:
+                quantise_attn(step)
+                turn_back(step)
 
         for m in range(M_TILES):
             result = results.tile([P, C], F32, name="result")

@@ -24,6 +24,7 @@ RUNS = SIDE // PACK
 HALVES = 2
 HALF_C = C // HALVES
 WORDS = HALF_C // 2
+SHORT = 3
 
 FLOPS = 2 * SIDE * SIDE * F * C
 BYTES = SIDE * SIDE * (F + C) * 2 + F * C * 4
@@ -73,6 +74,8 @@ def tile_windowattentionblock_pb_kernel(tc, attn_ctx, x, wo, bo, grad_out, out):
         nc.vector.tensor_copy(out=window_cols[:, :, :, 0], in_=image_cols[:, :, :, 1])
         nc.vector.tensor_copy(out=window_cols[:, 0 : GRID - 1, :, 1], in_=image_cols[:, 1:GRID, :, 0])
         nc.vector.tensor_copy(out=window_cols[:, GRID - 1, :, 1], in_=image_cols[:, 0, :, 0])
+        to_window_bf16 = const.tile([P, P], BF16)
+        nc.vector.tensor_copy(out=to_window_bf16[:], in_=to_window[:])
 
         a_codes = keep.tile([P, PASSES, F], U32, align_bytes=64)
         a_scales = keep.tile([P, PASSES, F], U8, align_bytes=64)
@@ -84,27 +87,42 @@ def tile_windowattentionblock_pb_kernel(tc, attn_ctx, x, wo, bo, grad_out, out):
         a_grouped = {}
         g_grouped = {}
 
+        def first_long(h):
+            return (SHORT - h + HALVES - 1) // HALVES
+
         def turn(gi):
             words = g_raw[gi][:].bitcast(F32).rearrange("p (j h w) -> p j h w", j=PACK, h=HALVES)
             g_turned[gi] = turned.tile([P, HALVES, PACK, P], F32, name="g_turned")
             for h in range(HALVES):
                 bank = psum.tile([P, PACK, P], F32, name="turn%d" % h)
-                for j in range(PACK):
+                for j in range(first_long(h), PACK):
                     nc.tensor.transpose(bank[:, j, :], words[:, j, h, :], to_window[:])
                 if h == 0:
-                    nc.vector.tensor_copy(out=g_turned[gi][:, h], in_=bank[:])
+                    nc.vector.tensor_copy(out=g_turned[gi][:, h, first_long(h) :], in_=bank[:, first_long(h) :])
                 else:
-                    nc.scalar.copy(out=g_turned[gi][:, h], in_=bank[:])
+                    nc.scalar.copy(out=g_turned[gi][:, h, first_long(h) :], in_=bank[:, first_long(h) :])
 
         def turn_back(gi):
+            pixels = g_raw[gi][:].rearrange("p (j h c) -> p j h c", j=PACK, h=HALVES)
             g_grouped[gi] = grouped.tile([P, C, PACK], BF16, name="g_grouped", align_bytes=64)
+            banks = [psum.tile([P, PACK, P], F32, name="back%d" % h) for h in range(HALVES)]
             for h in range(HALVES):
-                bank = psum.tile([P, PACK, P], F32, name="back%d" % h)
-                for j in range(PACK):
-                    nc.tensor.transpose(bank[:, j, :], g_turned[gi][:, h, j, :], identity[:])
-                nc.scalar.copy(
+                for j in range(first_long(h)):
+                    nc.tensor.matmul(
+                        out=banks[h][:, j, :].bitcast(BF16),
+                        lhsT=to_window_bf16[:],
+                        rhs=pixels[:, j, h, :],
+                        start=True,
+                        stop=True,
+                    )
+            for h in range(HALVES):
+                for j in range(first_long(h), PACK):
+                    nc.tensor.transpose(banks[h][:, j, :], g_turned[gi][:, h, j, :], identity[:])
+            for h in range(HALVES):
+                copier = nc.vector.tensor_copy if (gi == PASSES - 1 and h == 1) else nc.scalar.copy
+                copier(
                     out=g_grouped[gi][:, h * HALF_C : (h + 1) * HALF_C, :],
-                    in_=bank[:].bitcast(BF16).rearrange("p j c -> p c j"),
+                    in_=banks[h][:].bitcast(BF16).rearrange("p j c -> p c j"),
                 )
 
         def regroup_attn(gi):

@@ -115,7 +115,6 @@ def tile_windowattentionblock_pb_kernel(tc, attn_ctx, x, wo, bo, grad_out, out):
                         start=True,
                         stop=True,
                     )
-            for h in range(HALVES):
                 for j in range(first_long(h), PACK):
                     nc.tensor.transpose(banks[h][:, j, :], g_turned[gi][:, h, j, :], identity[:])
             for h in range(HALVES):

@@ -88,7 +88,7 @@ def tile_windowattentionblock_pb_kernel(tc, attn_ctx, x, wo, bo, grad_out, out):
         g_grouped = {}
 
         def first_long(h):
-            return (SHORT - h + HALVES - 1) // HALVES
+            return (SHORT - (1 - h) + HALVES - 1) // HALVES
 
         def turn(gi):
             words = g_raw[gi][:].bitcast(F32).rearrange("p (j h w) -> p j h w", j=PACK, h=HALVES)

@@ -24,7 +24,6 @@ RUNS = SIDE // PACK
 HALVES = 2
 HALF_C = C // HALVES
 WORDS = HALF_C // 2
-SHORT = 3
 
 FLOPS = 2 * SIDE * SIDE * F * C
 BYTES = SIDE * SIDE * (F + C) * 2 + F * C * 4
@@ -87,27 +86,31 @@ def tile_windowattentionblock_pb_kernel(tc, attn_ctx, x, wo, bo, grad_out, out):
         a_grouped = {}
         g_grouped = {}
 
-        def first_long(h):
-            return (SHORT - (1 - h) + HALVES - 1) // HALVES
+        def first_long(gi, h):
+            if gi == PASSES - 1:
+                return PACK
+            return 1 if h == 0 else 1 + gi % 2
 
         def turn(gi):
+            if gi == PASSES - 1:
+                return
             words = g_raw[gi][:].bitcast(F32).rearrange("p (j h w) -> p j h w", j=PACK, h=HALVES)
             g_turned[gi] = turned.tile([P, HALVES, PACK, P], F32, name="g_turned")
             for h in range(HALVES):
                 bank = psum.tile([P, PACK, P], F32, name="turn%d" % h)
-                for j in range(first_long(h), PACK):
+                for j in range(first_long(gi, h), PACK):
                     nc.tensor.transpose(bank[:, j, :], words[:, j, h, :], to_window[:])
                 if h == 0:
-                    nc.vector.tensor_copy(out=g_turned[gi][:, h, first_long(h) :], in_=bank[:, first_long(h) :])
+                    nc.vector.tensor_copy(out=g_turned[gi][:, h, first_long(gi, h) :], in_=bank[:, first_long(gi, h) :])
                 else:
-                    nc.scalar.copy(out=g_turned[gi][:, h, first_long(h) :], in_=bank[:, first_long(h) :])
+                    nc.scalar.copy(out=g_turned[gi][:, h, first_long(gi, h) :], in_=bank[:, first_long(gi, h) :])
 
         def turn_back(gi):
             pixels = g_raw[gi][:].rearrange("p (j h c) -> p j h c", j=PACK, h=HALVES)
             g_grouped[gi] = grouped.tile([P, C, PACK], BF16, name="g_grouped", align_bytes=64)
             banks = [psum.tile([P, PACK, P], F32, name="back%d" % h) for h in range(HALVES)]
             for h in range(HALVES):
-                for j in range(first_long(h)):
+                for j in range(first_long(gi, h)):
                     nc.tensor.matmul(
                         out=banks[h][:, j, :].bitcast(BF16),
                         lhsT=to_window_bf16[:],
@@ -115,11 +118,10 @@ def tile_windowattentionblock_pb_kernel(tc, attn_ctx, x, wo, bo, grad_out, out):
                         start=True,
                         stop=True,
                     )
-                for j in range(first_long(h), PACK):
+                for j in range(first_long(gi, h), PACK):
                     nc.tensor.transpose(banks[h][:, j, :], g_turned[gi][:, h, j, :], identity[:])
             for h in range(HALVES):
-                copier = nc.vector.tensor_copy if (gi == PASSES - 1 and h == 1) else nc.scalar.copy
-                copier(
+                nc.scalar.copy(
                     out=g_grouped[gi][:, h * HALF_C : (h + 1) * HALF_C, :],
                     in_=banks[h][:].bitcast(BF16).rearrange("p j c -> p c j"),
                 )

@@ -20,6 +20,7 @@ F = 512
 C = 512
 PASSES = GRID
 M_TILES = F // P
+SHORT_PASSES = 3
 RUNS = SIDE // PACK
 HALVES = 2
 HALF_C = C // HALVES
@@ -87,12 +88,10 @@ def tile_windowattentionblock_pb_kernel(tc, attn_ctx, x, wo, bo, grad_out, out):
         g_grouped = {}
 
         def first_long(gi, h):
-            if gi == PASSES - 1:
-                return PACK
-            return 1 if h == 0 else 1 + gi % 2
+            return PACK if gi < SHORT_PASSES else 0
 
         def turn(gi):
-            if gi == PASSES - 1:
+            if gi < SHORT_PASSES:
                 return
             words = g_raw[gi][:].bitcast(F32).rearrange("p (j h w) -> p j h w", j=PACK, h=HALVES)
             g_turned[gi] = turned.tile([P, HALVES, PACK, P], F32, name="g_turned")

@@ -109,6 +109,8 @@ def tile_windowattentionblock_pb_kernel(tc, attn_ctx, x, wo, bo, grad_out, out):
             g_grouped[gi] = grouped.tile([P, C, PACK], BF16, name="g_grouped", align_bytes=64)
             banks = [psum.tile([P, PACK, P], F32, name="back%d" % h) for h in range(HALVES)]
             for h in range(HALVES):
+                if h == 1 and 0 <= gi - 3:
+                    multiply(gi - 3, range(M_TILES // 2, M_TILES))
                 for j in range(first_long(gi, h)):
                     nc.tensor.matmul(
                         out=banks[h][:, j, :].bitcast(BF16),
@@ -146,8 +148,8 @@ def tile_windowattentionblock_pb_kernel(tc, attn_ctx, x, wo, bo, grad_out, out):
                 in_=g_grouped[gi][:].rearrange("p c j -> p (c j)"),
             )
 
-        def multiply(gi):
-            for m in range(M_TILES):
+        def multiply(gi, m_tiles):
+            for m in m_tiles:
                 f_cols = slice(m * P, (m + 1) * P)
                 nc.tensor.matmul_mx(
                     out=acc[m][:],
@@ -163,7 +165,7 @@ def tile_windowattentionblock_pb_kernel(tc, attn_ctx, x, wo, bo, grad_out, out):
             if step < PASSES:
                 turn(step)
             if 0 <= step - 3 < PASSES:
-                multiply(step - 3)
+                multiply(step - 3, range(M_TILES // 2 if step < PASSES else M_TILES))
             if step < PASSES:
                 regroup_attn(step)
             if 0 <= step - 1 < PASSES:

@@ -20,6 +20,8 @@ F = 512
 C = 512
 PASSES = GRID
 M_TILES = F // P
+ROW_BLOCKS = ((0, 0, WS),)
+WRAP_BLOCKS = ((0, 2, 4), (4, 0, 2), (6, 6, 2))
 SHORT_PASSES = 3
 RUNS = SIDE // PACK
 HALVES = 2
@@ -50,16 +52,11 @@ def tile_windowattentionblock_pb_kernel(tc, attn_ctx, x, wo, bo, grad_out, out):
         g_raw = []
         for gi in range(PASSES):
             g_tile = raw.tile([P, PACK * C], BF16, name="g_raw")
-            first = (gi * WS + SHIFT) % SIDE
-            head = min(WS, SIDE - first)
-            nc.sync.dma_start(
-                out=g_tile[0 : head * RUNS, :],
-                in_=image_runs[first : first + head].rearrange("i q e -> (i q) e"),
-            )
-            if head < WS:
+            for ti, block, rows in ROW_BLOCKS if gi < PASSES - 1 else WRAP_BLOCKS:
+                first = (gi * WS + SHIFT + ti) % SIDE
                 nc.sync.dma_start(
-                    out=g_tile[head * RUNS : P, :],
-                    in_=image_runs[0 : WS - head].rearrange("i q e -> (i q) e"),
+                    out=g_tile[block * RUNS : (block + rows) * RUNS, :],
+                    in_=image_runs[first : first + rows].rearrange("i q e -> (i q) e"),
                 )
             g_raw.append(g_tile)
             a_tile = raw.tile([P, PACK, F], BF16, name="a_raw")
@@ -68,12 +65,21 @@ def tile_windowattentionblock_pb_kernel(tc, attn_ctx, x, wo, bo, grad_out, out):
 
         identity = const.tile([P, P], F32)
         make_identity(nc, identity[:])
-        to_window = const.tile([P, P], F32)
-        image_cols = identity[:].rearrange("k (ti g e) -> k g ti e", g=GRID, e=2)
-        window_cols = to_window[:].rearrange("k (gj ti th) -> k gj ti th", ti=WS, th=2)
-        nc.vector.tensor_copy(out=window_cols[:, :, :, 0], in_=image_cols[:, :, :, 1])
-        nc.vector.tensor_copy(out=window_cols[:, 0 : GRID - 1, :, 1], in_=image_cols[:, 1:GRID, :, 0])
-        nc.vector.tensor_copy(out=window_cols[:, GRID - 1, :, 1], in_=image_cols[:, 0, :, 0])
+        image_cols = identity[:].rearrange("k (b g e) -> k g b e", g=GRID, e=2)
+
+        def window_matrix(engine, blocks, name):
+            matrix = const.tile([P, P], F32, name=name)
+            window_cols = matrix[:].rearrange("k (gj ti th) -> k gj ti th", ti=WS, th=2)
+            for ti, block, rows in blocks:
+                wanted = slice(ti, ti + rows)
+                held = slice(block, block + rows)
+                engine.tensor_copy(out=window_cols[:, :, wanted, 0], in_=image_cols[:, :, held, 1])
+                engine.tensor_copy(out=window_cols[:, 0 : GRID - 1, wanted, 1], in_=image_cols[:, 1:GRID, held, 0])
+                engine.tensor_copy(out=window_cols[:, GRID - 1, wanted, 1], in_=image_cols[:, 0, held, 0])
+            return matrix
+
+        to_window = window_matrix(nc.vector, ROW_BLOCKS, "to_window")
+        wrap_to_window = window_matrix(nc.gpsimd, WRAP_BLOCKS, "wrap_to_window")
         to_window_bf16 = const.tile([P, P], BF16)
         nc.vector.tensor_copy(out=to_window_bf16[:], in_=to_window[:])
 
@@ -95,10 +101,11 @@ def tile_windowattentionblock_pb_kernel(tc, attn_ctx, x, wo, bo, grad_out, out):
                 return
             words = g_raw[gi][:].bitcast(F32).rearrange("p (j h w) -> p j h w", j=PACK, h=HALVES)
             g_turned[gi] = turned.tile([P, HALVES, PACK, P], F32, name="g_turned")
+            matrix = to_window if gi < PASSES - 1 else wrap_to_window
             for h in range(HALVES):
                 bank = psum.tile([P, PACK, P], F32, name="turn%d" % h)
                 for j in range(first_long(gi, h), PACK):
-                    nc.tensor.transpose(bank[:, j, :], words[:, j, h, :], to_window[:])
+                    nc.tensor.transpose(bank[:, j, :], words[:, j, h, :], matrix[:])
                 if h == 0:
                     nc.vector.tensor_copy(out=g_turned[gi][:, h, first_long(gi, h) :], in_=bank[:, first_long(gi, h) :])
                 else:

@@ -173,18 +173,21 @@ def tile_windowattentionblock_pb_kernel(tc, attn_ctx, x, wo, bo, grad_out, out):
                 turn(step)
             if 0 <= step - 3 < PASSES:
                 multiply(step - 3, range(M_TILES // 2 if step < PASSES else M_TILES))
+            if 0 <= step - 1 < PASSES:
+                quantise_attn(step - 1)
             if step < PASSES:
                 regroup_attn(step)
             if 0 <= step - 1 < PASSES:
                 quantise_grad(step - 1)
             if step < PASSES:
-                quantise_attn(step)
                 turn_back(step)
 
         for m in range(M_TILES):
-            result = results.tile([P, C], F32, name="result")
-            if m % 2 == 0:
-                nc.scalar.copy(out=result[:], in_=acc[m][:])
-            else:
-                nc.vector.tensor_copy(out=result[:], in_=acc[m][:])
-            nc.sync.dma_start(out=out_rows[m * P : (m + 1) * P, :], in_=result[:])
+            copier = nc.scalar.copy if m % 2 == 0 else nc.vector.tensor_copy
+            pieces = 1 if m < M_TILES // 2 else 2
+            width = C // pieces
+            for n in range(pieces):
+                cols = slice(n * width, (n + 1) * width)
+                result = results.tile([P, width], F32, name="result%d" % pieces)
+                copier(out=result[:], in_=acc[m][:, cols])
+                nc.sync.dma_start(out=out_rows[m * P : (m + 1) * P, cols], in_=result[:])

from contextlib import ExitStack

import concourse.mybir as mybir
from concourse.masks import make_identity

BF16 = mybir.dt.bfloat16
F32 = mybir.dt.float32
U32 = mybir.dt.uint32
U8 = mybir.dt.uint8
E4M3X4 = mybir.dt.float8_e4m3fn_x4
E5M2X4 = mybir.dt.float8_e5m2_x4

P = 128
PACK = 4
SIDE = 64
WS = 8
SHIFT = 4
GRID = SIDE // WS
F = 512
C = 512
PASSES = GRID
M_TILES = F // P
ROW_BLOCKS = ((0, 0, WS),)
WRAP_BLOCKS = ((0, 2, 4), (4, 0, 2), (6, 6, 2))
SHORT_PASSES = 3
RUNS = SIDE // PACK
HALVES = 2
HALF_C = C // HALVES
WORDS = HALF_C // 2

FLOPS = 2 * SIDE * SIDE * F * C
BYTES = SIDE * SIDE * (F + C) * 2 + F * C * 4


def tile_windowattentionblock_pb_kernel(tc, attn_ctx, x, wo, bo, grad_out, out):
    nc = tc.nc
    attn_rows = attn_ctx.rearrange("(gi gj) (y j) h d -> gi (gj y) (j h d)", gj=GRID, j=PACK)
    image_runs = grad_out[0].rearrange("i (q j) c -> i q (j c)", j=PACK)
    out_rows = out.rearrange("h d c -> (h d) c")

    with ExitStack() as ctx:
        ctx.enter_context(tc.manual_schedule())
        const = ctx.enter_context(tc.tile_pool(name="const", bufs=1))
        raw = ctx.enter_context(tc.tile_pool(name="raw", bufs=PASSES))
        turned = ctx.enter_context(tc.tile_pool(name="turned", bufs=2))
        grouped = ctx.enter_context(tc.tile_pool(name="grouped", bufs=3))
        keep = ctx.enter_context(tc.tile_pool(name="keep", bufs=1))
        psum = ctx.enter_context(tc.psum_pool(name="psum", bufs=1))
        results = ctx.enter_context(tc.tile_pool(name="results", bufs=M_TILES))

        a_raw = []
        g_raw = []
        for gi in range(PASSES):
            g_tile = raw.tile([P, PACK * C], BF16, name="g_raw")
            for ti, block, rows in ROW_BLOCKS if gi < PASSES - 1 else WRAP_BLOCKS:
                first = (gi * WS + SHIFT + ti) % SIDE
                nc.sync.dma_start(
                    out=g_tile[block * RUNS : (block + rows) * RUNS, :],
                    in_=image_runs[first : first + rows].rearrange("i q e -> (i q) e"),
                )
            g_raw.append(g_tile)
            a_tile = raw.tile([P, PACK, F], BF16, name="a_raw")
            nc.sync.dma_start(out=a_tile[:].rearrange("p j f -> p (j f)"), in_=attn_rows[gi])
            a_raw.append(a_tile)

        identity = const.tile([P, P], F32)
        make_identity(nc, identity[:])
        image_cols = identity[:].rearrange("k (b g e) -> k g b e", g=GRID, e=2)

        def window_matrix(engine, blocks, name):
            matrix = const.tile([P, P], F32, name=name)
            window_cols = matrix[:].rearrange("k (gj ti th) -> k gj ti th", ti=WS, th=2)
            for ti, block, rows in blocks:
                wanted = slice(ti, ti + rows)
                held = slice(block, block + rows)
                engine.tensor_copy(out=window_cols[:, :, wanted, 0], in_=image_cols[:, :, held, 1])
                engine.tensor_copy(out=window_cols[:, 0 : GRID - 1, wanted, 1], in_=image_cols[:, 1:GRID, held, 0])
                engine.tensor_copy(out=window_cols[:, GRID - 1, wanted, 1], in_=image_cols[:, 0, held, 0])
            return matrix

        to_window = window_matrix(nc.vector, ROW_BLOCKS, "to_window")
        wrap_to_window = window_matrix(nc.gpsimd, WRAP_BLOCKS, "wrap_to_window")
        to_window_bf16 = const.tile([P, P], BF16)
        nc.vector.tensor_copy(out=to_window_bf16[:], in_=to_window[:])

        a_codes = keep.tile([P, PASSES, F], U32, align_bytes=64)
        a_scales = keep.tile([P, PASSES, F], U8, align_bytes=64)
        g_codes = keep.tile([P, PASSES, C], U32, align_bytes=64)
        g_scales = keep.tile([P, PASSES, C], U8, align_bytes=64)
        acc = [psum.tile([P, C], F32, name="acc%d" % m) for m in range(M_TILES)]

        g_turned = {}
        a_grouped = {}
        g_grouped = {}

        def first_long(gi, h):
            return PACK if gi < SHORT_PASSES else 0

        def turn(gi):
            if gi < SHORT_PASSES:
                return
            words = g_raw[gi][:].bitcast(F32).rearrange("p (j h w) -> p j h w", j=PACK, h=HALVES)
            g_turned[gi] = turned.tile([P, HALVES, PACK, P], F32, name="g_turned")
            matrix = to_window if gi < PASSES - 1 else wrap_to_window
            for h in range(HALVES):
                bank = psum.tile([P, PACK, P], F32, name="turn%d" % h)
                for j in range(first_long(gi, h), PACK):
                    nc.tensor.transpose(bank[:, j, :], words[:, j, h, :], matrix[:])
                if h == 0:
                    nc.vector.tensor_copy(out=g_turned[gi][:, h, first_long(gi, h) :], in_=bank[:, first_long(gi, h) :])
                else:
                    nc.scalar.copy(out=g_turned[gi][:, h, first_long(gi, h) :], in_=bank[:, first_long(gi, h) :])

        def turn_back(gi):
            pixels = g_raw[gi][:].rearrange("p (j h c) -> p j h c", j=PACK, h=HALVES)
            g_grouped[gi] = grouped.tile([P, C, PACK], BF16, name="g_grouped", align_bytes=64)
            banks = [psum.tile([P, PACK, P], F32, name="back%d" % h) for h in range(HALVES)]
            for h in range(HALVES):
                if h == 1 and 0 <= gi - 3:
                    multiply(gi - 3, range(M_TILES // 2, M_TILES))
                for j in range(first_long(gi, h)):
                    nc.tensor.matmul(
                        out=banks[h][:, j, :].bitcast(BF16),
                        lhsT=to_window_bf16[:],
                        rhs=pixels[:, j, h, :],
                        start=True,
                        stop=True,
                    )
                for j in range(first_long(gi, h), PACK):
                    nc.tensor.transpose(banks[h][:, j, :], g_turned[gi][:, h, j, :], identity[:])
            for h in range(HALVES):
                nc.scalar.copy(
                    out=g_grouped[gi][:, h * HALF_C : (h + 1) * HALF_C, :],
                    in_=banks[h][:].bitcast(BF16).rearrange("p j c -> p c j"),
                )

        def regroup_attn(gi):
            a_grouped[gi] = grouped.tile([P, F, PACK], BF16, name="a_grouped", align_bytes=64)
            nc.vector.tensor_copy(
                out=a_grouped[gi][:].rearrange("p (b i) j -> p b j i", i=4),
                in_=a_raw[gi][:].rearrange("p j (b i) -> p b j i", i=4),
            )

        def quantise_attn(gi):
            nc.vector.quantize_mx(
                out=a_codes[:, gi, :].bitcast(E4M3X4),
                scales=a_scales[:, gi, :],
                in_=a_grouped[gi][:].rearrange("p f j -> p (f j)"),
            )

        def quantise_grad(gi):
            nc.vector.quantize_mx(
                out=g_codes[:, gi, :].bitcast(E5M2X4),
                scales=g_scales[:, gi, :],
                in_=g_grouped[gi][:].rearrange("p c j -> p (c j)"),
            )

        def multiply(gi, m_tiles):
            for m in m_tiles:
                f_cols = slice(m * P, (m + 1) * P)
                nc.tensor.matmul_mx(
                    out=acc[m][:],
                    lhsT=a_codes[:, gi, f_cols].bitcast(E4M3X4),
                    lhsT_scale=a_scales[:, gi, f_cols],
                    rhs=g_codes[:, gi, :].bitcast(E5M2X4),
                    rhs_scale=g_scales[:, gi, :],
                    start=(gi == 0),
                    stop=(gi == PASSES - 1),
                )

        for step in range(PASSES + 3):
            if step < PASSES:
                turn(step)
            if 0 <= step - 3 < PASSES:
                multiply(step - 3, range(M_TILES // 2 if step < PASSES else M_TILES))
            if 0 <= step - 1 < PASSES:
                quantise_attn(step - 1)
            if step < PASSES:
                regroup_attn(step)
            if 0 <= step - 1 < PASSES:
                quantise_grad(step - 1)
            if step < PASSES:
                turn_back(step)

        for m in range(M_TILES):
            copier = nc.scalar.copy if m % 2 == 0 else nc.vector.tensor_copy
            pieces = 1 if m < M_TILES // 2 else 2
            width = C // pieces
            for n in range(pieces):
                cols = slice(n * width, (n + 1) * width)
                result = results.tile([P, width], F32, name="result%d" % pieces)
                copier(out=result[:], in_=acc[m][:, cols])
                nc.sync.dma_start(out=out_rows[m * P : (m + 1) * P, cols], in_=result[:])
